import numpy as np
import ml_dtypes


def mxq(x, axis, fmt="e4m3"):
    dtype, down = {"e4m3": (ml_dtypes.float8_e4m3fn, 7), "e5m2": (ml_dtypes.float8_e5m2, 14)}[fmt]
    v = np.moveaxis(np.asarray(x, np.float32).astype(ml_dtypes.bfloat16).astype(np.float64), axis, -1)
    blocks = v.reshape(v.shape[:-1] + (-1, 32))
    amax = np.abs(blocks).max(-1, keepdims=True)
    byte = np.maximum(np.where(amax > 0, np.frexp(amax)[1] - 1 + 127, 0) - down, 1)
    scale = np.exp2(byte - 127.0)
    codes = (blocks / scale).astype(np.float32).astype(dtype).astype(np.float64)
    return np.moveaxis((codes * scale).reshape(v.shape), -1, axis)


WIDE = False


def mx_kscale(k):
    if not WIDE:
        return np.ones(k)
    levels = np.array([10, -10, 5, -5, 0])
    a = np.random.permutation(np.resize(levels, k // 512 * 4)).reshape(k // 512, 4)
    idx = np.arange(k)
    return np.exp2(a[idx // 512, idx % 128 // 32])


BF16 = ml_dtypes.bfloat16


def bf(x):
    return np.asarray(x, np.float32).astype(BF16)


def f64(x):
    return np.asarray(x).astype(np.float64)


E2M1 = np.array([0.0, 0.5, 1.0, 1.5, 2.0, 3.0, 4.0, 6.0, -0.0, -0.5, -1.0, -1.5, -2.0, -3.0, -4.0, -6.0])


def pack_weight(w, fmt):
    k, n = w.shape
    w = f64(bf(w)).reshape(k // 32, 32, n)
    amax = np.abs(w).max(1)
    if fmt == "e4m3":
        byte = np.frexp(amax)[1] - 1 + 127 - 7
    else:
        mant, ex = np.frexp(amax / 6.0)
        byte = np.where(mant > 0.5, ex, ex - 1) + 127
    byte = np.clip(np.where(amax > 0, byte, 1), 1, 254)
    scaled = (w * np.exp2(127.0 - byte)[:, None, :]).reshape(k, n).astype(np.float32)
    by_word = np.ascontiguousarray(scaled.reshape(k // 512, 128, 4, n).transpose(0, 1, 3, 2))
    if fmt == "e4m3":
        words = by_word.astype(ml_dtypes.float8_e4m3fn).view(np.uint8)
    else:
        c = by_word.astype(ml_dtypes.float4_e2m1fn).view(np.uint8) & 0xF
        words = c[..., 0::2] | (c[..., 1::2] << 4)
    return np.ascontiguousarray(words), np.ascontiguousarray(byte.astype(np.uint8).reshape(k // 512, 16, n))


def unpack_weight(words, scales, fmt):
    g, p, n, _ = words.shape
    if fmt == "e4m3":
        vals = np.ascontiguousarray(words).view(ml_dtypes.float8_e4m3fn).astype(np.float64)
    else:
        nib = np.empty((g, p, n, 4), np.uint8)
        nib[..., 0::2] = words & 0xF
        nib[..., 1::2] = words >> 4
        vals = E2M1[nib]
    vals = vals * np.repeat(np.exp2(scales.astype(np.float64) - 127.0), 8, axis=1)[..., None]
    return vals.transpose(0, 1, 3, 2).reshape(g * 512, n)

def pack4(w):
    words, scales = pack_weight(w, "e2m1")
    return words.reshape(words.shape[0], 128, -1), scales


def unpack4(words, scales):
    return unpack_weight(words.reshape(words.shape[0], 128, -1, 2), scales, "e2m1")


B, T, C, H, NOPE, ROPE, VD, LORA = 4, 1024, 1024, 4, 128, 128, 128, 512
QK = NOPE + ROPE
HALF = ROPE // 2


def make_freq_cis():
    inv = 1.0 / (10000.0 ** (np.arange(0, ROPE, 2) / ROPE))
    ang = np.outer(np.arange(T), inv)
    return np.stack([np.cos(ang), np.sin(ang)], -1)


def apply_rope(v, fc):
    vr = v.reshape(B, T, H, HALF, 2)
    f = fc.reshape(1, T, 1, HALF, 2)
    real = vr[..., 0] * f[..., 0] - vr[..., 1] * f[..., 1]
    imag = vr[..., 1] * f[..., 0] + vr[..., 0] * f[..., 1]
    return np.stack([real, imag], -1).reshape(B, T, H, ROPE)


def setup_inputs():
    s = mx_kscale(C)
    x = bf(np.random.standard_normal((B, T, C)) * s)
    freq_cis = bf(make_freq_cis())
    words, scales = pack4(np.random.standard_normal((C, H * QK)) * 2.0 / np.sqrt(C) / s[:, None])
    return {"x": x,
            "freq_cis": freq_cis,
            "Wq_words": words,
            "Wq_scales": scales}


def reference(x, freq_cis, Wq_words, Wq_scales):
    q = (mxq(f64(x), 2, "e4m3") @ unpack4(Wq_words, Wq_scales)).reshape(B, T, H, QK)
    q_nope, q_rope = q[..., :NOPE], q[..., NOPE:]
    q_rope = apply_rope(q_rope, f64(freq_cis))
    return np.concatenate([q_nope, q_rope], -1)

@@ -1,0 +1,184 @@
+from contextlib import ExitStack
+
+import concourse.mybir as mybir
+from concourse.masks import make_identity
+
+F32 = mybir.dt.float32
+BF16 = mybir.dt.bfloat16
+I32 = mybir.dt.int32
+U32 = mybir.dt.uint32
+U8 = mybir.dt.uint8
+FP8X4 = mybir.dt.float8_e4m3fn_x4
+FP4X4 = mybir.dt.float4_e2m1fn_x4
+MULT = mybir.AluOpType.mult
+ADD = mybir.AluOpType.add
+
+P = 128
+BATCH, SEQ, C = 4, 1024, 1024
+HEADS, NOPE, ROPE = 4, 128, 128
+PAIRS = ROPE // 2
+K_PASS = 4 * P
+PASSES = C // K_PASS
+BANK = 512
+PSUM_BANKS = 8
+TILES_PER_BATCH = SEQ // P
+TILES_PER_ROUND = 2
+ROUNDS = BATCH * TILES_PER_BATCH // TILES_PER_ROUND
+ROUNDS_PER_BATCH = TILES_PER_BATCH // TILES_PER_ROUND
+KEPT, ROTATED = 0, 1
+
+FLOPS = 2 * BATCH * SEQ * C * HEADS * (NOPE + ROPE)
+
+
+def tile_multiheadlatentattention_pb_t_kernel(tc, x, freq_cis, Wq_words, Wq_scales, out):
+    nc = tc.nc
+    with ExitStack() as ctx:
+        ctx.enter_context(tc.manual_schedule())
+        keep = ctx.enter_context(tc.tile_pool(name="keep", bufs=1))
+        stage = ctx.enter_context(tc.tile_pool(name="stage", bufs=2))
+        halves = ctx.enter_context(tc.tile_pool(name="halves", bufs=3))
+        results = ctx.enter_context(tc.tile_pool(name="results", bufs=10))
+        flipped = ctx.enter_context(tc.psum_pool(name="flipped", bufs=TILES_PER_ROUND))
+        sums = ctx.enter_context(tc.psum_pool(name="sums", bufs=PSUM_BANKS - TILES_PER_ROUND))
+
+        x_by_tile = x.rearrange("b (p j) k -> b p j k", j=TILES_PER_BATCH)
+        out_by_tile = out.rearrange("b (p j) h d -> b p j (h d)", j=TILES_PER_BATCH)
+
+        identity = keep.tile([P, P], F32)
+        make_identity(nc, identity[:])
+
+        x_rounds = []
+
+        def load_x(r):
+            b, first = divmod(r * TILES_PER_ROUND, TILES_PER_BATCH)
+            x_sb = keep.tile([P, TILES_PER_ROUND, C], BF16, name="x%d" % r)
+            nc.sync.dma_start(out=x_sb[:], in_=x_by_tile[b, :, first : first + TILES_PER_ROUND, :])
+            x_rounds.append(x_sb)
+
+        load_x(0)
+
+        scales_in = keep.tile([P, PASSES, HEADS * (NOPE + ROPE)], U8, align_bytes=64)
+        nc.vector.memset(scales_in[:].bitcast(I32), 0)
+        for quadrant in range(4):
+            nc.sync.dma_start(
+                out=scales_in[32 * quadrant : 32 * quadrant + 4].bitcast(I32),
+                in_=Wq_scales[:, 4 * quadrant : 4 * quadrant + 4, :].bitcast(I32).rearrange("g r n -> r g n"),
+            )
+
+        w_words = keep.tile([P, PASSES, 2, 2 * BANK], U8, align_bytes=64)
+        for g in range(PASSES):
+            by_half = Wq_words[g].bitcast(I32).rearrange("p (h f c) -> p f h c", h=HEADS, f=2)
+            for f in (ROTATED, KEPT):
+                nc.sync.dma_start(
+                    out=w_words[:, g, f, :].bitcast(I32).rearrange("p (h c) -> p h c", h=HEADS),
+                    in_=by_half[:, f],
+                )
+        load_x(1)
+
+        from_even_by = keep.tile([P, TILES_PER_BATCH, ROPE], BF16)
+        nc.sync.dma_start(
+            out=from_even_by[:], in_=freq_cis.rearrange("(p j) i e -> p j (i e)", j=TILES_PER_BATCH)
+        )
+        for r in range(2, ROUNDS):
+            load_x(r)
+
+        w_scales = keep.tile([P, PASSES, 2, BANK], U8, align_bytes=64)
+        for g in range(PASSES):
+            nc.vector.tensor_copy(
+                out=w_scales[:, g].rearrange("p f n -> p (f n)").bitcast(I32).rearrange(
+                    "p (f h c) -> p f h c", f=2, h=HEADS
+                ),
+                in_=scales_in[:, g, :].bitcast(I32).rearrange("p (h f c) -> p f h c", h=HEADS, f=2),
+            )
+
+        grouped_of = {}
+        codes_of = {}
+
+        def transpose_round(r):
+            x_words = x_rounds[r][:].bitcast(F32)
+            grouped = stage.tile([P, TILES_PER_ROUND, C], BF16, align_bytes=64, name="grouped")
+            for a in range(TILES_PER_ROUND):
+                xt = flipped.tile([P, 2 * PASSES, P], F32, name="xt")
+                for g in range(PASSES):
+                    for u in range(2):
+                        nc.tensor.transpose(
+                            xt[:, 2 * g + u, :],
+                            x_words[:, a, 256 * g + u : 256 * (g + 1) : 2],
+                            identity[:],
+                        )
+                nc.scalar.copy(
+                    out=grouped[:, a, :].bitcast(F32).rearrange("p (g r u) -> p g r u", g=PASSES, u=2),
+                    in_=xt[:].rearrange("p (g u) r -> p g r u", u=2),
+                )
+            grouped_of[r] = grouped
+
+        def quantise_round(r):
+            codes = stage.tile([P, TILES_PER_ROUND * PASSES * P], U32, align_bytes=64, name="codes")
+            x_scales = stage.tile([P, TILES_PER_ROUND * PASSES * P], U8, align_bytes=64, name="x_scales")
+            nc.vector.quantize_mx(
+                out=codes[:].bitcast(FP8X4),
+                scales=x_scales[:],
+                in_=grouped_of[r][:].rearrange("p a c -> p (a c)"),
+            )
+            codes_of[r] = (codes, x_scales)
+
+        def multiply(r, a, f):
+            codes, x_scales = codes_of[r]
+            acc = sums.tile([P, BANK], F32, name="acc")
+            for g in range(PASSES):
+                tokens = slice((a * PASSES + g) * P, (a * PASSES + g + 1) * P)
+                nc.tensor.matmul_mx(
+                    out=acc[:],
+                    lhsT=codes[:, tokens].bitcast(FP8X4),
+                    lhsT_scale=x_scales[:, tokens],
+                    rhs=w_words[:, g, f, :].bitcast(FP4X4),
+                    rhs_scale=w_scales[:, g, f, :],
+                    start=(g == 0),
+                    stop=(g == PASSES - 1),
+                )
+            return acc
+
+        def finish(r, a, kept, rotated):
+            b, j = divmod(r * TILES_PER_ROUND + a, TILES_PER_BATCH)
+            result = results.tile([P, HEADS, NOPE + ROPE], F32, name="result")
+            nc.scalar.copy(out=result[:, :, :NOPE], in_=kept[:].rearrange("p (h d) -> p h d", h=HEADS))
+            shape = [P, HEADS, PAIRS, 2]
+            pairs = rotated[:].rearrange("p (h i e) -> p h i e", h=HEADS, e=2)
+            from_even = halves.tile([P, HEADS, ROPE], F32, name="from_even")
+            from_odd = halves.tile([P, HEADS, ROPE], F32, name="from_odd")
+            nc.vector.tensor_tensor(
+                out=from_even[:].rearrange("p h (i e) -> p h i e", e=2),
+                in0=pairs[:, :, :, 0:1].to_broadcast(shape),
+                in1=from_even_by[:, j, :].rearrange("p (i e) -> p i e", e=2).unsqueeze(1).to_broadcast(shape),
+                op=MULT,
+            )
+            nc.vector.tensor_tensor(
+                out=from_odd[:].rearrange("p h (i e) -> p h i e", e=2),
+                in0=pairs[:, :, :, 1:2].to_broadcast(shape),
+                in1=from_odd_by[:, j, :].rearrange("p (i e) -> p i e", e=2).unsqueeze(1).to_broadcast(shape),
+                op=MULT,
+            )
+            nc.gpsimd.tensor_tensor(out=result[:, :, NOPE:], in0=from_even[:], in1=from_odd[:], op=ADD)
+            nc.sync.dma_start(out=out_by_tile[b, :, j, :], in_=result[:].rearrange("p h d -> p (h d)"))
+
+        transpose_round(0)
+        quantise_round(0)
+
+        from_odd_by = keep.tile([P, TILES_PER_BATCH, ROPE], BF16)
+        cos_sin = from_even_by[:].rearrange("p j (i e) -> p (j i) e", e=2)
+        sin_cos = from_odd_by[:].rearrange("p j (i e) -> p (j i) e", e=2)
+        nc.vector.tensor_scalar_mul(out=sin_cos[:, :, 0:1], in0=cos_sin[:, :, 1:2], scalar1=-1.0)
+        nc.vector.tensor_copy(out=sin_cos[:, :, 1:2], in_=cos_sin[:, :, 0:1])
+
+        for r in range(ROUNDS):
+            if r + 1 < ROUNDS:
+                transpose_round(r + 1)
+            banks = []
+            for a in range(TILES_PER_ROUND):
+                rotated = multiply(r, a, ROTATED)
+                kept = multiply(r, a, KEPT)
+                banks.append((kept, rotated))
+            if r + 1 < ROUNDS:
+                quantise_round(r + 1)
+            for a in range(TILES_PER_ROUND):
+                finish(r, a, banks[a][0], banks[a][1])

@@ -26,6 +26,8 @@ TILES_PER_ROUND = 2
 ROUNDS = BATCH * TILES_PER_BATCH // TILES_PER_ROUND
 ROUNDS_PER_BATCH = TILES_PER_BATCH // TILES_PER_ROUND
 KEPT, ROTATED = 0, 1
+TILES = ROUNDS * TILES_PER_ROUND
+SORTED_PASSES = 1
 
 FLOPS = 2 * BATCH * SEQ * C * HEADS * (NOPE + ROPE)
 
@@ -36,6 +38,7 @@ def tile_multiheadlatentattention_pb_t_kernel(tc, x, freq_cis, Wq_words, Wq_scal
         ctx.enter_context(tc.manual_schedule())
         keep = ctx.enter_context(tc.tile_pool(name="keep", bufs=1))
         stage = ctx.enter_context(tc.tile_pool(name="stage", bufs=2))
+        sorting = ctx.enter_context(tc.tile_pool(name="sorting", bufs=3 * TILES_PER_ROUND))
         halves = ctx.enter_context(tc.tile_pool(name="halves", bufs=3))
         results = ctx.enter_context(tc.tile_pool(name="results", bufs=10))
         flipped = ctx.enter_context(tc.psum_pool(name="flipped", bufs=TILES_PER_ROUND))
@@ -93,19 +96,31 @@ def tile_multiheadlatentattention_pb_t_kernel(tc, x, freq_cis, Wq_words, Wq_scal
 
         grouped_of = {}
         codes_of = {}
+        sorted_of = {}
+
+        def sort_words(tile):
+            r, a = divmod(tile, TILES_PER_ROUND)
+            in_order = sorting.tile([P, SORTED_PASSES, 2, P], F32, name="in_order")
+            nc.scalar.copy(
+                out=in_order[:],
+                in_=x_rounds[r][:].bitcast(F32)[:, a, : 256 * SORTED_PASSES].rearrange(
+                    "p (g q u) -> p g u q", g=SORTED_PASSES, u=2
+                ),
+            )
+            sorted_of[tile] = in_order
 
         def transpose_round(r):
             x_words = x_rounds[r][:].bitcast(F32)
             grouped = stage.tile([P, TILES_PER_ROUND, C], BF16, align_bytes=64, name="grouped")
             for a in range(TILES_PER_ROUND):
                 xt = flipped.tile([P, 2 * PASSES, P], F32, name="xt")
-                for g in range(PASSES):
+                for g in reversed(range(PASSES)):
                     for u in range(2):
-                        nc.tensor.transpose(
-                            xt[:, 2 * g + u, :],
-                            x_words[:, a, 256 * g + u : 256 * (g + 1) : 2],
-                            identity[:],
-                        )
+                        if g < SORTED_PASSES:
+                            words = sorted_of[r * TILES_PER_ROUND + a][:, g, u, :]
+                        else:
+                            words = x_words[:, a, 256 * g + u : 256 * (g + 1) : 2]
+                        nc.tensor.transpose(xt[:, 2 * g + u, :], words, identity[:])
                 nc.scalar.copy(
                     out=grouped[:, a, :].bitcast(F32).rearrange("p (g r u) -> p g r u", g=PASSES, u=2),
                     in_=xt[:].rearrange("p (g u) r -> p g r u", u=2),
@@ -158,10 +173,15 @@ def tile_multiheadlatentattention_pb_t_kernel(tc, x, freq_cis, Wq_words, Wq_scal
                 in1=from_odd_by[:, j, :].rearrange("p (i e) -> p i e", e=2).unsqueeze(1).to_broadcast(shape),
                 op=MULT,
             )
-            nc.gpsimd.tensor_tensor(out=result[:, :, NOPE:], in0=from_even[:], in1=from_odd[:], op=ADD)
+            adder = nc.vector if r * TILES_PER_ROUND + a == TILES - 1 else nc.gpsimd
+            adder.tensor_tensor(out=result[:, :, NOPE:], in0=from_even[:], in1=from_odd[:], op=ADD)
             nc.sync.dma_start(out=out_by_tile[b, :, j, :], in_=result[:].rearrange("p h d -> p (h d)"))
 
+        for tile in range(TILES_PER_ROUND):
+            sort_words(tile)
         transpose_round(0)
+        for tile in range(TILES_PER_ROUND, 2 * TILES_PER_ROUND):
+            sort_words(tile)
         quantise_round(0)
 
         from_odd_by = keep.tile([P, TILES_PER_BATCH, ROPE], BF16)
@@ -181,4 +201,6 @@ def tile_multiheadlatentattention_pb_t_kernel(tc, x, freq_cis, Wq_words, Wq_scal
             if r + 1 < ROUNDS:
                 quantise_round(r + 1)
             for a in range(TILES_PER_ROUND):
+                if r + 2 < ROUNDS:
+                    sort_words((r + 2) * TILES_PER_ROUND + a)
                 finish(r, a, banks[a][0], banks[a][1])

@@ -26,8 +26,6 @@ TILES_PER_ROUND = 2
 ROUNDS = BATCH * TILES_PER_BATCH // TILES_PER_ROUND
 ROUNDS_PER_BATCH = TILES_PER_BATCH // TILES_PER_ROUND
 KEPT, ROTATED = 0, 1
-TILES = ROUNDS * TILES_PER_ROUND
-SORTED_PASSES = 1
 
 FLOPS = 2 * BATCH * SEQ * C * HEADS * (NOPE + ROPE)
 
@@ -38,7 +36,6 @@ def tile_multiheadlatentattention_pb_t_kernel(tc, x, freq_cis, Wq_words, Wq_scal
         ctx.enter_context(tc.manual_schedule())
         keep = ctx.enter_context(tc.tile_pool(name="keep", bufs=1))
         stage = ctx.enter_context(tc.tile_pool(name="stage", bufs=2))
-        sorting = ctx.enter_context(tc.tile_pool(name="sorting", bufs=3 * TILES_PER_ROUND))
         halves = ctx.enter_context(tc.tile_pool(name="halves", bufs=3))
         results = ctx.enter_context(tc.tile_pool(name="results", bufs=10))
         flipped = ctx.enter_context(tc.psum_pool(name="flipped", bufs=TILES_PER_ROUND))
@@ -59,6 +56,7 @@ def tile_multiheadlatentattention_pb_t_kernel(tc, x, freq_cis, Wq_words, Wq_scal
             x_rounds.append(x_sb)
 
         load_x(0)
+        load_x(1)
 
         scales_in = keep.tile([P, PASSES, HEADS * (NOPE + ROPE)], U8, align_bytes=64)
         nc.vector.memset(scales_in[:].bitcast(I32), 0)
@@ -76,7 +74,6 @@ def tile_multiheadlatentattention_pb_t_kernel(tc, x, freq_cis, Wq_words, Wq_scal
                     out=w_words[:, g, f, :].bitcast(I32).rearrange("p (h c) -> p h c", h=HEADS),
                     in_=by_half[:, f],
                 )
-        load_x(1)
 
         from_even_by = keep.tile([P, TILES_PER_BATCH, ROPE], BF16)
         nc.sync.dma_start(
@@ -96,31 +93,19 @@ def tile_multiheadlatentattention_pb_t_kernel(tc, x, freq_cis, Wq_words, Wq_scal
 
         grouped_of = {}
         codes_of = {}
-        sorted_of = {}
-
-        def sort_words(tile):
-            r, a = divmod(tile, TILES_PER_ROUND)
-            in_order = sorting.tile([P, SORTED_PASSES, 2, P], F32, name="in_order")
-            nc.scalar.copy(
-                out=in_order[:],
-                in_=x_rounds[r][:].bitcast(F32)[:, a, : 256 * SORTED_PASSES].rearrange(
-                    "p (g q u) -> p g u q", g=SORTED_PASSES, u=2
-                ),
-            )
-            sorted_of[tile] = in_order
 
         def transpose_round(r):
             x_words = x_rounds[r][:].bitcast(F32)
             grouped = stage.tile([P, TILES_PER_ROUND, C], BF16, align_bytes=64, name="grouped")
             for a in range(TILES_PER_ROUND):
                 xt = flipped.tile([P, 2 * PASSES, P], F32, name="xt")
-                for g in reversed(range(PASSES)):
+                for g in range(PASSES):
                     for u in range(2):
-                        if g < SORTED_PASSES:
-                            words = sorted_of[r * TILES_PER_ROUND + a][:, g, u, :]
-                        else:
-                            words = x_words[:, a, 256 * g + u : 256 * (g + 1) : 2]
-                        nc.tensor.transpose(xt[:, 2 * g + u, :], words, identity[:])
+                        nc.tensor.transpose(
+                            xt[:, 2 * g + u, :],
+                            x_words[:, a, 256 * g + u : 256 * (g + 1) : 2],
+                            identity[:],
+                        )
                 nc.scalar.copy(
                     out=grouped[:, a, :].bitcast(F32).rearrange("p (g r u) -> p g r u", g=PASSES, u=2),
                     in_=xt[:].rearrange("p (g u) r -> p g r u", u=2),
@@ -173,15 +158,10 @@ def tile_multiheadlatentattention_pb_t_kernel(tc, x, freq_cis, Wq_words, Wq_scal
                 in1=from_odd_by[:, j, :].rearrange("p (i e) -> p i e", e=2).unsqueeze(1).to_broadcast(shape),
                 op=MULT,
             )
-            adder = nc.vector if r * TILES_PER_ROUND + a == TILES - 1 else nc.gpsimd
-            adder.tensor_tensor(out=result[:, :, NOPE:], in0=from_even[:], in1=from_odd[:], op=ADD)
+            nc.gpsimd.tensor_tensor(out=result[:, :, NOPE:], in0=from_even[:], in1=from_odd[:], op=ADD)
             nc.sync.dma_start(out=out_by_tile[b, :, j, :], in_=result[:].rearrange("p h d -> p (h d)"))
 
-        for tile in range(TILES_PER_ROUND):
-            sort_words(tile)
         transpose_round(0)
-        for tile in range(TILES_PER_ROUND, 2 * TILES_PER_ROUND):
-            sort_words(tile)
         quantise_round(0)
 
         from_odd_by = keep.tile([P, TILES_PER_BATCH, ROPE], BF16)
@@ -201,6 +181,4 @@ def tile_multiheadlatentattention_pb_t_kernel(tc, x, freq_cis, Wq_words, Wq_scal
             if r + 1 < ROUNDS:
                 quantise_round(r + 1)
             for a in range(TILES_PER_ROUND):
-                if r + 2 < ROUNDS:
-                    sort_words((r + 2) * TILES_PER_ROUND + a)
                 finish(r, a, banks[a][0], banks[a][1])

@@ -26,6 +26,8 @@ TILES_PER_ROUND = 2
 ROUNDS = BATCH * TILES_PER_BATCH // TILES_PER_ROUND
 ROUNDS_PER_BATCH = TILES_PER_BATCH // TILES_PER_ROUND
 KEPT, ROTATED = 0, 1
+SORT_AHEAD = 3
+SORTED_PASSES = (2, 1)
 
 FLOPS = 2 * BATCH * SEQ * C * HEADS * (NOPE + ROPE)
 
@@ -36,6 +38,7 @@ def tile_multiheadlatentattention_pb_t_kernel(tc, x, freq_cis, Wq_words, Wq_scal
         ctx.enter_context(tc.manual_schedule())
         keep = ctx.enter_context(tc.tile_pool(name="keep", bufs=1))
         stage = ctx.enter_context(tc.tile_pool(name="stage", bufs=2))
+        sorting = ctx.enter_context(tc.tile_pool(name="sorting", bufs=SORT_AHEAD + 1))
         halves = ctx.enter_context(tc.tile_pool(name="halves", bufs=3))
         results = ctx.enter_context(tc.tile_pool(name="results", bufs=10))
         flipped = ctx.enter_context(tc.psum_pool(name="flipped", bufs=TILES_PER_ROUND))
@@ -93,6 +96,18 @@ def tile_multiheadlatentattention_pb_t_kernel(tc, x, freq_cis, Wq_words, Wq_scal
 
         grouped_of = {}
         codes_of = {}
+        sorted_of = {}
+
+        def sort_words(r, a):
+            if r >= ROUNDS:
+                return
+            words = 256 * SORTED_PASSES[a]
+            sorted_words = sorting.tile([P, words], F32, name="sorted%d" % a)
+            nc.scalar.copy(
+                out=sorted_words[:].rearrange("p (g u w) -> p g u w", u=2, w=P),
+                in_=x_rounds[r][:].bitcast(F32)[:, a, :words].rearrange("p (g w u) -> p g u w", u=2, w=P),
+            )
+            sorted_of[(r, a)] = sorted_words
 
         def transpose_round(r):
             x_words = x_rounds[r][:].bitcast(F32)
@@ -101,11 +116,11 @@ def tile_multiheadlatentattention_pb_t_kernel(tc, x, freq_cis, Wq_words, Wq_scal
                 xt = flipped.tile([P, 2 * PASSES, P], F32, name="xt")
                 for g in range(PASSES):
                     for u in range(2):
-                        nc.tensor.transpose(
-                            xt[:, 2 * g + u, :],
-                            x_words[:, a, 256 * g + u : 256 * (g + 1) : 2],
-                            identity[:],
-                        )
+                        if (r, a) in sorted_of and g < SORTED_PASSES[a]:
+                            columns = sorted_of[(r, a)][:, (2 * g + u) * P : (2 * g + u + 1) * P]
+                        else:
+                            columns = x_words[:, a, 256 * g + u : 256 * (g + 1) : 2]
+                        nc.tensor.transpose(xt[:, 2 * g + u, :], columns, identity[:])
                 nc.scalar.copy(
                     out=grouped[:, a, :].bitcast(F32).rearrange("p (g r u) -> p g r u", g=PASSES, u=2),
                     in_=xt[:].rearrange("p (g u) r -> p g r u", u=2),
@@ -138,10 +153,22 @@ def tile_multiheadlatentattention_pb_t_kernel(tc, x, freq_cis, Wq_words, Wq_scal
                 )
             return acc
 
-        def finish(r, a, kept, rotated):
+        LAST = ROUNDS - 1
+
+        def place_in_out(r, a):
             b, j = divmod(r * TILES_PER_ROUND + a, TILES_PER_BATCH)
+            rows = out_by_tile[b, :, j, :]
+            return j, rows, rows.rearrange("p (h f d) -> p h f d", h=HEADS, f=2)
+
+        def copy_kept(r, a, kept):
             result = results.tile([P, HEADS, NOPE + ROPE], F32, name="result")
             nc.scalar.copy(out=result[:, :, :NOPE], in_=kept[:].rearrange("p (h d) -> p h d", h=HEADS))
+            if r == LAST:
+                nc.sync.dma_start(out=place_in_out(r, a)[2][:, :, KEPT, :], in_=result[:, :, :NOPE])
+            return result
+
+        def rotate(r, a, rotated, result):
+            j, rows, place = place_in_out(r, a)
             shape = [P, HEADS, PAIRS, 2]
             pairs = rotated[:].rearrange("p (h i e) -> p h i e", h=HEADS, e=2)
             from_even = halves.tile([P, HEADS, ROPE], F32, name="from_even")
@@ -158,8 +185,18 @@ def tile_multiheadlatentattention_pb_t_kernel(tc, x, freq_cis, Wq_words, Wq_scal
                 in1=from_odd_by[:, j, :].rearrange("p (i e) -> p i e", e=2).unsqueeze(1).to_broadcast(shape),
                 op=MULT,
             )
-            nc.gpsimd.tensor_tensor(out=result[:, :, NOPE:], in0=from_even[:], in1=from_odd[:], op=ADD)
-            nc.sync.dma_start(out=out_by_tile[b, :, j, :], in_=result[:].rearrange("p h d -> p (h d)"))
+            if (r, a) != (LAST, TILES_PER_ROUND - 1):
+                nc.gpsimd.tensor_tensor(out=result[:, :, NOPE:], in0=from_even[:], in1=from_odd[:], op=ADD)
+                if r == LAST:
+                    nc.sync.dma_start(out=place[:, :, ROTATED, :], in_=result[:, :, NOPE:])
+                else:
+                    nc.sync.dma_start(out=rows, in_=result[:].rearrange("p h d -> p (h d)"))
+                return
+            for h in range(0, HEADS, 2):
+                nc.vector.tensor_tensor(
+                    out=result[:, h : h + 2, NOPE:], in0=from_even[:, h : h + 2, :], in1=from_odd[:, h : h + 2, :], op=ADD
+                )
+                nc.sync.dma_start(out=place[:, h : h + 2, ROTATED, :], in_=result[:, h : h + 2, NOPE:])
 
         transpose_round(0)
         quantise_round(0)
@@ -173,6 +210,7 @@ def tile_multiheadlatentattention_pb_t_kernel(tc, x, freq_cis, Wq_words, Wq_scal
         for r in range(ROUNDS):
             if r + 1 < ROUNDS:
                 transpose_round(r + 1)
+            sort_words(r + SORT_AHEAD, 1)
             banks = []
             for a in range(TILES_PER_ROUND):
                 rotated = multiply(r, a, ROTATED)
@@ -180,5 +218,8 @@ def tile_multiheadlatentattention_pb_t_kernel(tc, x, freq_cis, Wq_words, Wq_scal
                 banks.append((kept, rotated))
             if r + 1 < ROUNDS:
                 quantise_round(r + 1)
+            whole = [copy_kept(r, 0, banks[0][0])]
+            sort_words(r + SORT_AHEAD, 0)
+            whole.append(copy_kept(r, 1, banks[1][0]))
             for a in range(TILES_PER_ROUND):
-                finish(r, a, banks[a][0], banks[a][1])
+                rotate(r, a, banks[a][1], whole[a])

@@ -78,10 +78,8 @@ def tile_multiheadlatentattention_pb_t_kernel(tc, x, freq_cis, Wq_words, Wq_scal
                     in_=by_half[:, f],
                 )
 
-        from_even_by = keep.tile([P, TILES_PER_BATCH, ROPE], BF16)
-        nc.sync.dma_start(
-            out=from_even_by[:], in_=freq_cis.rearrange("(p j) i e -> p j (i e)", j=TILES_PER_BATCH)
-        )
+        cos_sin = keep.tile([P, TILES_PER_BATCH * PAIRS, 2], BF16)
+        nc.sync.dma_start(out=cos_sin[:], in_=freq_cis.rearrange("(p j) i e -> p (j i) e", j=TILES_PER_BATCH))
         for r in range(2, ROUNDS):
             load_x(r)
 
@@ -169,24 +167,18 @@ def tile_multiheadlatentattention_pb_t_kernel(tc, x, freq_cis, Wq_words, Wq_scal
 
         def rotate(r, a, rotated, result):
             j, rows, place = place_in_out(r, a)
-            shape = [P, HEADS, PAIRS, 2]
-            pairs = rotated[:].rearrange("p (h i e) -> p h i e", h=HEADS, e=2)
-            from_even = halves.tile([P, HEADS, ROPE], F32, name="from_even")
-            from_odd = halves.tile([P, HEADS, ROPE], F32, name="from_odd")
+            shape = [P, HEADS, ROPE, 2]
+            products = halves.tile(shape, F32, name="products")
             nc.vector.tensor_tensor(
-                out=from_even[:].rearrange("p h (i e) -> p h i e", e=2),
-                in0=pairs[:, :, :, 0:1].to_broadcast(shape),
-                in1=from_even_by[:, j, :].rearrange("p (i e) -> p i e", e=2).unsqueeze(1).to_broadcast(shape),
+                out=products[:],
+                in0=rotated[:].rearrange("p (h m) -> p h m", h=HEADS).unsqueeze(3).to_broadcast(shape),
+                in1=factors[:, j].unsqueeze(1).to_broadcast(shape),
                 op=MULT,
             )
-            nc.vector.tensor_tensor(
-                out=from_odd[:].rearrange("p h (i e) -> p h i e", e=2),
-                in0=pairs[:, :, :, 1:2].to_broadcast(shape),
-                in1=from_odd_by[:, j, :].rearrange("p (i e) -> p i e", e=2).unsqueeze(1).to_broadcast(shape),
-                op=MULT,
-            )
+            by_pair = products[:].rearrange("p h (i q) e -> p h i q e", q=2)
+            turned = result[:, :, NOPE:].rearrange("p h (i e) -> p h i e", e=2)
             if (r, a) != (LAST, TILES_PER_ROUND - 1):
-                nc.gpsimd.tensor_tensor(out=result[:, :, NOPE:], in0=from_even[:], in1=from_odd[:], op=ADD)
+                nc.gpsimd.tensor_tensor(out=turned, in0=by_pair[:, :, :, 0, :], in1=by_pair[:, :, :, 1, :], op=ADD)
                 if r == LAST:
                     nc.sync.dma_start(out=place[:, :, ROTATED, :], in_=result[:, :, NOPE:])
                 else:
@@ -194,21 +186,25 @@ def tile_multiheadlatentattention_pb_t_kernel(tc, x, freq_cis, Wq_words, Wq_scal
                 return
             for h in range(0, HEADS, 2):
                 nc.vector.tensor_tensor(
-                    out=result[:, h : h + 2, NOPE:], in0=from_even[:, h : h + 2, :], in1=from_odd[:, h : h + 2, :], op=ADD
+                    out=turned[:, h : h + 2],
+                    in0=by_pair[:, h : h + 2, :, 0, :],
+                    in1=by_pair[:, h : h + 2, :, 1, :],
+                    op=ADD,
                 )
                 nc.sync.dma_start(out=place[:, h : h + 2, ROTATED, :], in_=result[:, h : h + 2, NOPE:])
 
         transpose_round(0)
         quantise_round(0)
+        transpose_round(1)
 
-        from_odd_by = keep.tile([P, TILES_PER_BATCH, ROPE], BF16)
-        cos_sin = from_even_by[:].rearrange("p j (i e) -> p (j i) e", e=2)
-        sin_cos = from_odd_by[:].rearrange("p j (i e) -> p (j i) e", e=2)
-        nc.vector.tensor_scalar_mul(out=sin_cos[:, :, 0:1], in0=cos_sin[:, :, 1:2], scalar1=-1.0)
-        nc.vector.tensor_copy(out=sin_cos[:, :, 1:2], in_=cos_sin[:, :, 0:1])
+        factors = keep.tile([P, TILES_PER_BATCH, ROPE, 2], BF16)
+        by_q = factors[:].rearrange("p j (i q) e -> p (j i) q e", q=2)
+        nc.scalar.copy(out=by_q[:, :, 0, :], in_=cos_sin[:])
+        nc.vector.tensor_scalar_mul(out=by_q[:, :, 1, 0:1], in0=cos_sin[:, :, 1:2], scalar1=-1.0)
+        nc.vector.tensor_copy(out=by_q[:, :, 1, 1:2], in_=cos_sin[:, :, 0:1])
 
         for r in range(ROUNDS):
-            if r + 1 < ROUNDS:
+            if 1 <= r < ROUNDS - 1:
                 transpose_round(r + 1)
             sort_words(r + SORT_AHEAD, 1)
             banks = []

@@ -40,7 +40,7 @@ def tile_multiheadlatentattention_pb_t_kernel(tc, x, freq_cis, Wq_words, Wq_scal
         stage = ctx.enter_context(tc.tile_pool(name="stage", bufs=2))
         sorting = ctx.enter_context(tc.tile_pool(name="sorting", bufs=SORT_AHEAD + 1))
         halves = ctx.enter_context(tc.tile_pool(name="halves", bufs=3))
-        results = ctx.enter_context(tc.tile_pool(name="results", bufs=10))
+        results = ctx.enter_context(tc.tile_pool(name="results", bufs=6))
         flipped = ctx.enter_context(tc.psum_pool(name="flipped", bufs=TILES_PER_ROUND))
         sums = ctx.enter_context(tc.psum_pool(name="sums", bufs=PSUM_BANKS - TILES_PER_ROUND))
 
@@ -152,46 +152,57 @@ def tile_multiheadlatentattention_pb_t_kernel(tc, x, freq_cis, Wq_words, Wq_scal
             return acc
 
         LAST = ROUNDS - 1
+        HEADS_OF_ROUND = TILES_PER_ROUND * HEADS
 
-        def place_in_out(r, a):
-            b, j = divmod(r * TILES_PER_ROUND + a, TILES_PER_BATCH)
-            rows = out_by_tile[b, :, j, :]
-            return j, rows, rows.rearrange("p (h f d) -> p h f d", h=HEADS, f=2)
+        def heads_of(a):
+            return slice(a * HEADS, (a + 1) * HEADS)
 
-        def copy_kept(r, a, kept):
-            result = results.tile([P, HEADS, NOPE + ROPE], F32, name="result")
-            nc.scalar.copy(out=result[:, :, :NOPE], in_=kept[:].rearrange("p (h d) -> p h d", h=HEADS))
-            if r == LAST:
-                nc.sync.dma_start(out=place_in_out(r, a)[2][:, :, KEPT, :], in_=result[:, :, :NOPE])
-            return result
+        def copy_kept(a, kept, result):
+            nc.scalar.copy(out=result[:, heads_of(a), :NOPE], in_=kept[:].rearrange("p (h d) -> p h d", h=HEADS))
 
-        def rotate(r, a, rotated, result):
-            j, rows, place = place_in_out(r, a)
+        def multiply_by_factors(r, a, rotated, products):
+            j = (r * TILES_PER_ROUND + a) % TILES_PER_BATCH
             shape = [P, HEADS, ROPE, 2]
-            products = halves.tile(shape, F32, name="products")
             nc.vector.tensor_tensor(
-                out=products[:],
+                out=products[:, heads_of(a)],
                 in0=rotated[:].rearrange("p (h m) -> p h m", h=HEADS).unsqueeze(3).to_broadcast(shape),
                 in1=factors[:, j].unsqueeze(1).to_broadcast(shape),
                 op=MULT,
             )
-            by_pair = products[:].rearrange("p h (i q) e -> p h i q e", q=2)
-            turned = result[:, :, NOPE:].rearrange("p h (i e) -> p h i e", e=2)
-            if (r, a) != (LAST, TILES_PER_ROUND - 1):
-                nc.gpsimd.tensor_tensor(out=turned, in0=by_pair[:, :, :, 0, :], in1=by_pair[:, :, :, 1, :], op=ADD)
-                if r == LAST:
-                    nc.sync.dma_start(out=place[:, :, ROTATED, :], in_=result[:, :, NOPE:])
-                else:
-                    nc.sync.dma_start(out=rows, in_=result[:].rearrange("p h d -> p (h d)"))
+
+        def add_products(engine, heads, products, result):
+            by_pair = products[:, heads].rearrange("p t (i q) e -> p t i q e", q=2)
+            engine.tensor_tensor(
+                out=result[:, heads, NOPE:].rearrange("p t (i e) -> p t i e", e=2),
+                in0=by_pair[:, :, :, 0, :],
+                in1=by_pair[:, :, :, 1, :],
+                op=ADD,
+            )
+
+        def add_and_store(r, products, result):
+            b, first = divmod(r * TILES_PER_ROUND, TILES_PER_BATCH)
+            if r < LAST - 1:
+                add_products(nc.gpsimd, slice(0, HEADS_OF_ROUND), products, result)
+                nc.sync.dma_start(
+                    out=out_by_tile[b, :, first : first + TILES_PER_ROUND, :],
+                    in_=result[:].rearrange("p (a h) d -> p a (h d)", h=HEADS),
+                )
+                return
+            for a in range(TILES_PER_ROUND):
+                if (r, a) != (LAST, TILES_PER_ROUND - 1):
+                    add_products(nc.gpsimd, heads_of(a), products, result)
+                    nc.sync.dma_start(
+                        out=out_by_tile[b, :, first + a, :], in_=result[:, heads_of(a)].rearrange("p h d -> p (h d)")
+                    )
+            if r != LAST:
                 return
             for h in range(0, HEADS, 2):
-                nc.vector.tensor_tensor(
-                    out=turned[:, h : h + 2],
-                    in0=by_pair[:, h : h + 2, :, 0, :],
-                    in1=by_pair[:, h : h + 2, :, 1, :],
-                    op=ADD,
+                heads = slice(HEADS + h, HEADS + h + 2)
+                add_products(nc.vector, heads, products, result)
+                nc.sync.dma_start(
+                    out=out_by_tile[b, :, first + 1, h * (NOPE + ROPE) : (h + 2) * (NOPE + ROPE)],
+                    in_=result[:, heads].rearrange("p h d -> p (h d)"),
                 )
-                nc.sync.dma_start(out=place[:, h : h + 2, ROTATED, :], in_=result[:, h : h + 2, NOPE:])
 
         transpose_round(0)
         quantise_round(0)
@@ -214,8 +225,11 @@ def tile_multiheadlatentattention_pb_t_kernel(tc, x, freq_cis, Wq_words, Wq_scal
                 banks.append((kept, rotated))
             if r + 1 < ROUNDS:
                 quantise_round(r + 1)
-            whole = [copy_kept(r, 0, banks[0][0])]
+            result = results.tile([P, HEADS_OF_ROUND, NOPE + ROPE], F32, name="result")
+            products = halves.tile([P, HEADS_OF_ROUND, ROPE, 2], F32, name="products")
+            copy_kept(0, banks[0][0], result)
             sort_words(r + SORT_AHEAD, 0)
-            whole.append(copy_kept(r, 1, banks[1][0]))
+            copy_kept(1, banks[1][0], result)
             for a in range(TILES_PER_ROUND):
-                rotate(r, a, banks[a][1], whole[a])
+                multiply_by_factors(r, a, banks[a][1], products)
+            add_and_store(r, products, result)

@@ -26,7 +26,8 @@ TILES_PER_ROUND = 2
 ROUNDS = BATCH * TILES_PER_BATCH // TILES_PER_ROUND
 ROUNDS_PER_BATCH = TILES_PER_BATCH // TILES_PER_ROUND
 KEPT, ROTATED = 0, 1
-SORT_AHEAD = 3
+SORT_AHEAD = 4
+FIRST_SORTED = 6
 SORTED_PASSES = (2, 1)
 
 FLOPS = 2 * BATCH * SEQ * C * HEADS * (NOPE + ROPE)
@@ -38,6 +39,7 @@ def tile_multiheadlatentattention_pb_t_kernel(tc, x, freq_cis, Wq_words, Wq_scal
         ctx.enter_context(tc.manual_schedule())
         keep = ctx.enter_context(tc.tile_pool(name="keep", bufs=1))
         stage = ctx.enter_context(tc.tile_pool(name="stage", bufs=2))
+        ahead = ctx.enter_context(tc.tile_pool(name="ahead", bufs=3))
         sorting = ctx.enter_context(tc.tile_pool(name="sorting", bufs=SORT_AHEAD + 1))
         halves = ctx.enter_context(tc.tile_pool(name="halves", bufs=3))
         results = ctx.enter_context(tc.tile_pool(name="results", bufs=6))
@@ -97,7 +99,7 @@ def tile_multiheadlatentattention_pb_t_kernel(tc, x, freq_cis, Wq_words, Wq_scal
         sorted_of = {}
 
         def sort_words(r, a):
-            if r >= ROUNDS:
+            if r < FIRST_SORTED or r >= ROUNDS:
                 return
             words = 256 * SORTED_PASSES[a]
             sorted_words = sorting.tile([P, words], F32, name="sorted%d" % a)
@@ -109,7 +111,7 @@ def tile_multiheadlatentattention_pb_t_kernel(tc, x, freq_cis, Wq_words, Wq_scal
 
         def transpose_round(r):
             x_words = x_rounds[r][:].bitcast(F32)
-            grouped = stage.tile([P, TILES_PER_ROUND, C], BF16, align_bytes=64, name="grouped")
+            grouped = ahead.tile([P, TILES_PER_ROUND, C], BF16, align_bytes=64, name="grouped")
             for a in range(TILES_PER_ROUND):
                 xt = flipped.tile([P, 2 * PASSES, P], F32, name="xt")
                 for g in range(PASSES):
@@ -215,14 +217,16 @@ def tile_multiheadlatentattention_pb_t_kernel(tc, x, freq_cis, Wq_words, Wq_scal
         nc.vector.tensor_copy(out=by_q[:, :, 1, 1:2], in_=cos_sin[:, :, 0:1])
 
         for r in range(ROUNDS):
-            if 1 <= r < ROUNDS - 1:
-                transpose_round(r + 1)
+            if 2 <= r < ROUNDS - 2:
+                transpose_round(r + 2)
             sort_words(r + SORT_AHEAD, 1)
             banks = []
             for a in range(TILES_PER_ROUND):
                 rotated = multiply(r, a, ROTATED)
                 kept = multiply(r, a, KEPT)
                 banks.append((kept, rotated))
+                if (r, a) in ((0, 1), (1, 0)):
+                    transpose_round(r + 2)
             if r + 1 < ROUNDS:
                 quantise_round(r + 1)
             result = results.tile([P, HEADS_OF_ROUND, NOPE + ROPE], F32, name="result")

@@ -27,6 +27,7 @@ ROUNDS = BATCH * TILES_PER_BATCH // TILES_PER_ROUND
 ROUNDS_PER_BATCH = TILES_PER_BATCH // TILES_PER_ROUND
 KEPT, ROTATED = 0, 1
 SORT_AHEAD = 4
+FINE_ROUNDS = 4
 FIRST_SORTED = 6
 SORTED_PASSES = (2, 1)
 
@@ -57,7 +58,11 @@ def tile_multiheadlatentattention_pb_t_kernel(tc, x, freq_cis, Wq_words, Wq_scal
         def load_x(r):
             b, first = divmod(r * TILES_PER_ROUND, TILES_PER_BATCH)
             x_sb = keep.tile([P, TILES_PER_ROUND, C], BF16, name="x%d" % r)
-            nc.sync.dma_start(out=x_sb[:], in_=x_by_tile[b, :, first : first + TILES_PER_ROUND, :])
+            if r == 0:
+                for a in range(TILES_PER_ROUND):
+                    nc.sync.dma_start(out=x_sb[:, a, :], in_=x_by_tile[b, :, first + a, :])
+            else:
+                nc.sync.dma_start(out=x_sb[:], in_=x_by_tile[b, :, first : first + TILES_PER_ROUND, :])
             x_rounds.append(x_sb)
 
         load_x(0)
@@ -72,9 +77,9 @@ def tile_multiheadlatentattention_pb_t_kernel(tc, x, freq_cis, Wq_words, Wq_scal
             )
 
         w_words = keep.tile([P, PASSES, 2, 2 * BANK], U8, align_bytes=64)
-        for g in range(PASSES):
-            by_half = Wq_words[g].bitcast(I32).rearrange("p (h f c) -> p f h c", h=HEADS, f=2)
-            for f in (ROTATED, KEPT):
+        for f in (ROTATED, KEPT):
+            for g in range(PASSES):
+                by_half = Wq_words[g].bitcast(I32).rearrange("p (h f c) -> p f h c", h=HEADS, f=2)
                 nc.sync.dma_start(
                     out=w_words[:, g, f, :].bitcast(I32).rearrange("p (h c) -> p h c", h=HEADS),
                     in_=by_half[:, f],
@@ -130,11 +135,14 @@ def tile_multiheadlatentattention_pb_t_kernel(tc, x, freq_cis, Wq_words, Wq_scal
         def quantise_round(r):
             codes = stage.tile([P, TILES_PER_ROUND * PASSES * P], U32, align_bytes=64, name="codes")
             x_scales = stage.tile([P, TILES_PER_ROUND * PASSES * P], U8, align_bytes=64, name="x_scales")
-            nc.vector.quantize_mx(
-                out=codes[:].bitcast(FP8X4),
-                scales=x_scales[:],
-                in_=grouped_of[r][:].rearrange("p a c -> p (a c)"),
-            )
+            pieces = TILES_PER_ROUND if r == 0 else 1
+            width = TILES_PER_ROUND * PASSES * P // pieces
+            for i in range(pieces):
+                nc.vector.quantize_mx(
+                    out=codes[:, i * width : (i + 1) * width].bitcast(FP8X4),
+                    scales=x_scales[:, i * width : (i + 1) * width],
+                    in_=grouped_of[r][:].rearrange("p a c -> p (a c)")[:, 4 * i * width : 4 * (i + 1) * width],
+                )
             codes_of[r] = (codes, x_scales)
 
         def multiply(r, a, f):
@@ -183,7 +191,7 @@ def tile_multiheadlatentattention_pb_t_kernel(tc, x, freq_cis, Wq_words, Wq_scal
 
         def add_and_store(r, products, result):
             b, first = divmod(r * TILES_PER_ROUND, TILES_PER_BATCH)
-            if r < LAST - 1:
+            if r <= LAST - FINE_ROUNDS:
                 add_products(nc.gpsimd, slice(0, HEADS_OF_ROUND), products, result)
                 nc.sync.dma_start(
                     out=out_by_tile[b, :, first : first + TILES_PER_ROUND, :],
@@ -192,7 +200,7 @@ def tile_multiheadlatentattention_pb_t_kernel(tc, x, freq_cis, Wq_words, Wq_scal
                 return
             for a in range(TILES_PER_ROUND):
                 if (r, a) != (LAST, TILES_PER_ROUND - 1):
-                    add_products(nc.gpsimd, heads_of(a), products, result)
+                    add_products(nc.vector if r == LAST else nc.gpsimd, heads_of(a), products, result)
                     nc.sync.dma_start(
                         out=out_by_tile[b, :, first + a, :], in_=result[:, heads_of(a)].rearrange("p h d -> p (h d)")
                     )

@@ -68,7 +68,7 @@ def tile_multiheadlatentattention_pb_t_kernel(tc, x, freq_cis, Wq_words, Wq_scal
         load_x(0)
         load_x(1)
 
-        scales_in = keep.tile([P, PASSES, HEADS * (NOPE + ROPE)], U8, align_bytes=64)
+        scales_in = keep.tile([P, PASSES, HEADS * (NOPE + ROPE)], U8, align_bytes=256)
         nc.vector.memset(scales_in[:].bitcast(I32), 0)
         for quadrant in range(4):
             nc.sync.dma_start(
@@ -76,7 +76,7 @@ def tile_multiheadlatentattention_pb_t_kernel(tc, x, freq_cis, Wq_words, Wq_scal
                 in_=Wq_scales[:, 4 * quadrant : 4 * quadrant + 4, :].bitcast(I32).rearrange("g r n -> r g n"),
             )
 
-        w_words = keep.tile([P, PASSES, 2, 2 * BANK], U8, align_bytes=64)
+        w_words = keep.tile([P, PASSES, 2, 2 * BANK], U8, align_bytes=256)
         for f in (ROTATED, KEPT):
             for g in range(PASSES):
                 by_half = Wq_words[g].bitcast(I32).rearrange("p (h f c) -> p f h c", h=HEADS, f=2)
@@ -90,7 +90,7 @@ def tile_multiheadlatentattention_pb_t_kernel(tc, x, freq_cis, Wq_words, Wq_scal
         for r in range(2, ROUNDS):
             load_x(r)
 
-        w_scales = keep.tile([P, PASSES, 2, BANK], U8, align_bytes=64)
+        w_scales = keep.tile([P, PASSES, 2, BANK], U8, align_bytes=256)
         for g in range(PASSES):
             nc.vector.tensor_copy(
                 out=w_scales[:, g].rearrange("p f n -> p (f n)").bitcast(I32).rearrange(
@@ -116,7 +116,7 @@ def tile_multiheadlatentattention_pb_t_kernel(tc, x, freq_cis, Wq_words, Wq_scal
 
         def transpose_round(r):
             x_words = x_rounds[r][:].bitcast(F32)
-            grouped = ahead.tile([P, TILES_PER_ROUND, C], BF16, align_bytes=64, name="grouped")
+            grouped = ahead.tile([P, TILES_PER_ROUND, C], BF16, align_bytes=256, name="grouped")
             for a in range(TILES_PER_ROUND):
                 xt = flipped.tile([P, 2 * PASSES, P], F32, name="xt")
                 for g in range(PASSES):
@@ -133,8 +133,8 @@ def tile_multiheadlatentattention_pb_t_kernel(tc, x, freq_cis, Wq_words, Wq_scal
             grouped_of[r] = grouped
 
         def quantise_round(r):
-            codes = stage.tile([P, TILES_PER_ROUND * PASSES * P], U32, align_bytes=64, name="codes")
-            x_scales = stage.tile([P, TILES_PER_ROUND * PASSES * P], U8, align_bytes=64, name="x_scales")
+            codes = stage.tile([P, TILES_PER_ROUND * PASSES * P], U32, align_bytes=256, name="codes")
+            x_scales = stage.tile([P, TILES_PER_ROUND * PASSES * P], U8, align_bytes=256, name="x_scales")
             pieces = TILES_PER_ROUND if r == 0 else 1
             width = TILES_PER_ROUND * PASSES * P // pieces
             for i in range(pieces):

@@ -90,15 +90,6 @@ def tile_multiheadlatentattention_pb_t_kernel(tc, x, freq_cis, Wq_words, Wq_scal
         for r in range(2, ROUNDS):
             load_x(r)
 
-        w_scales = keep.tile([P, PASSES, 2, BANK], U8, align_bytes=256)
-        for g in range(PASSES):
-            nc.vector.tensor_copy(
-                out=w_scales[:, g].rearrange("p f n -> p (f n)").bitcast(I32).rearrange(
-                    "p (f h c) -> p f h c", f=2, h=HEADS
-                ),
-                in_=scales_in[:, g, :].bitcast(I32).rearrange("p (h f c) -> p f h c", h=HEADS, f=2),
-            )
-
         grouped_of = {}
         codes_of = {}
         sorted_of = {}
@@ -217,6 +208,15 @@ def tile_multiheadlatentattention_pb_t_kernel(tc, x, freq_cis, Wq_words, Wq_scal
         transpose_round(0)
         quantise_round(0)
         transpose_round(1)
+
+        w_scales = keep.tile([P, PASSES, 2, BANK], U8, align_bytes=256)
+        for g in range(PASSES):
+            nc.vector.tensor_copy(
+                out=w_scales[:, g].rearrange("p f n -> p (f n)").bitcast(I32).rearrange(
+                    "p (f h c) -> p f h c", f=2, h=HEADS
+                ),
+                in_=scales_in[:, g, :].bitcast(I32).rearrange("p (h f c) -> p f h c", h=HEADS, f=2),
+            )
 
         factors = keep.tile([P, TILES_PER_BATCH, ROPE, 2], BF16)
         by_q = factors[:].rearrange("p j (i q) e -> p (j i) q e", q=2)

from contextlib import ExitStack

import concourse.mybir as mybir
from concourse.masks import make_identity

F32 = mybir.dt.float32
BF16 = mybir.dt.bfloat16
I32 = mybir.dt.int32
U32 = mybir.dt.uint32
U8 = mybir.dt.uint8
FP8X4 = mybir.dt.float8_e4m3fn_x4
FP4X4 = mybir.dt.float4_e2m1fn_x4
MULT = mybir.AluOpType.mult
ADD = mybir.AluOpType.add

P = 128
BATCH, SEQ, C = 4, 1024, 1024
HEADS, NOPE, ROPE = 4, 128, 128
PAIRS = ROPE // 2
K_PASS = 4 * P
PASSES = C // K_PASS
BANK = 512
PSUM_BANKS = 8
TILES_PER_BATCH = SEQ // P
TILES_PER_ROUND = 2
ROUNDS = BATCH * TILES_PER_BATCH // TILES_PER_ROUND
ROUNDS_PER_BATCH = TILES_PER_BATCH // TILES_PER_ROUND
KEPT, ROTATED = 0, 1
SORT_AHEAD = 4
FINE_ROUNDS = 4
FIRST_SORTED = 6
SORTED_PASSES = (2, 1)

FLOPS = 2 * BATCH * SEQ * C * HEADS * (NOPE + ROPE)


def tile_multiheadlatentattention_pb_t_kernel(tc, x, freq_cis, Wq_words, Wq_scales, out):
    nc = tc.nc
    with ExitStack() as ctx:
        ctx.enter_context(tc.manual_schedule())
        keep = ctx.enter_context(tc.tile_pool(name="keep", bufs=1))
        stage = ctx.enter_context(tc.tile_pool(name="stage", bufs=2))
        ahead = ctx.enter_context(tc.tile_pool(name="ahead", bufs=3))
        sorting = ctx.enter_context(tc.tile_pool(name="sorting", bufs=SORT_AHEAD + 1))
        halves = ctx.enter_context(tc.tile_pool(name="halves", bufs=3))
        results = ctx.enter_context(tc.tile_pool(name="results", bufs=6))
        flipped = ctx.enter_context(tc.psum_pool(name="flipped", bufs=TILES_PER_ROUND))
        sums = ctx.enter_context(tc.psum_pool(name="sums", bufs=PSUM_BANKS - TILES_PER_ROUND))

        x_by_tile = x.rearrange("b (p j) k -> b p j k", j=TILES_PER_BATCH)
        out_by_tile = out.rearrange("b (p j) h d -> b p j (h d)", j=TILES_PER_BATCH)

        identity = keep.tile([P, P], F32)
        make_identity(nc, identity[:])

        x_rounds = []

        def load_x(r):
            b, first = divmod(r * TILES_PER_ROUND, TILES_PER_BATCH)
            x_sb = keep.tile([P, TILES_PER_ROUND, C], BF16, name="x%d" % r)
            if r == 0:
                for a in range(TILES_PER_ROUND):
                    nc.sync.dma_start(out=x_sb[:, a, :], in_=x_by_tile[b, :, first + a, :])
            else:
                nc.sync.dma_start(out=x_sb[:], in_=x_by_tile[b, :, first : first + TILES_PER_ROUND, :])
            x_rounds.append(x_sb)

        load_x(0)
        load_x(1)

        scales_in = keep.tile([P, PASSES, HEADS * (NOPE + ROPE)], U8, align_bytes=256)
        nc.vector.memset(scales_in[:].bitcast(I32), 0)
        for quadrant in range(4):
            nc.sync.dma_start(
                out=scales_in[32 * quadrant : 32 * quadrant + 4].bitcast(I32),
                in_=Wq_scales[:, 4 * quadrant : 4 * quadrant + 4, :].bitcast(I32).rearrange("g r n -> r g n"),
            )

        w_words = keep.tile([P, PASSES, 2, 2 * BANK], U8, align_bytes=256)
        for f in (ROTATED, KEPT):
            for g in range(PASSES):
                by_half = Wq_words[g].bitcast(I32).rearrange("p (h f c) -> p f h c", h=HEADS, f=2)
                nc.sync.dma_start(
                    out=w_words[:, g, f, :].bitcast(I32).rearrange("p (h c) -> p h c", h=HEADS),
                    in_=by_half[:, f],
                )

        cos_sin = keep.tile([P, TILES_PER_BATCH * PAIRS, 2], BF16)
        nc.sync.dma_start(out=cos_sin[:], in_=freq_cis.rearrange("(p j) i e -> p (j i) e", j=TILES_PER_BATCH))
        for r in range(2, ROUNDS):
            load_x(r)

        grouped_of = {}
        codes_of = {}
        sorted_of = {}

        def sort_words(r, a):
            if r < FIRST_SORTED or r >= ROUNDS:
                return
            words = 256 * SORTED_PASSES[a]
            sorted_words = sorting.tile([P, words], F32, name="sorted%d" % a)
            nc.scalar.copy(
                out=sorted_words[:].rearrange("p (g u w) -> p g u w", u=2, w=P),
                in_=x_rounds[r][:].bitcast(F32)[:, a, :words].rearrange("p (g w u) -> p g u w", u=2, w=P),
            )
            sorted_of[(r, a)] = sorted_words

        def transpose_round(r):
            x_words = x_rounds[r][:].bitcast(F32)
            grouped = ahead.tile([P, TILES_PER_ROUND, C], BF16, align_bytes=256, name="grouped")
            for a in range(TILES_PER_ROUND):
                xt = flipped.tile([P, 2 * PASSES, P], F32, name="xt")
                for g in range(PASSES):
                    for u in range(2):
                        if (r, a) in sorted_of and g < SORTED_PASSES[a]:
                            columns = sorted_of[(r, a)][:, (2 * g + u) * P : (2 * g + u + 1) * P]
                        else:
                            columns = x_words[:, a, 256 * g + u : 256 * (g + 1) : 2]
                        nc.tensor.transpose(xt[:, 2 * g + u, :], columns, identity[:])
                nc.scalar.copy(
                    out=grouped[:, a, :].bitcast(F32).rearrange("p (g r u) -> p g r u", g=PASSES, u=2),
                    in_=xt[:].rearrange("p (g u) r -> p g r u", u=2),
                )
            grouped_of[r] = grouped

        def quantise_round(r):
            codes = stage.tile([P, TILES_PER_ROUND * PASSES * P], U32, align_bytes=256, name="codes")
            x_scales = stage.tile([P, TILES_PER_ROUND * PASSES * P], U8, align_bytes=256, name="x_scales")
            pieces = TILES_PER_ROUND if r == 0 else 1
            width = TILES_PER_ROUND * PASSES * P // pieces
            for i in range(pieces):
                nc.vector.quantize_mx(
                    out=codes[:, i * width : (i + 1) * width].bitcast(FP8X4),
                    scales=x_scales[:, i * width : (i + 1) * width],
                    in_=grouped_of[r][:].rearrange("p a c -> p (a c)")[:, 4 * i * width : 4 * (i + 1) * width],
                )
            codes_of[r] = (codes, x_scales)

        def multiply(r, a, f):
            codes, x_scales = codes_of[r]
            acc = sums.tile([P, BANK], F32, name="acc")
            for g in range(PASSES):
                tokens = slice((a * PASSES + g) * P, (a * PASSES + g + 1) * P)
                nc.tensor.matmul_mx(
                    out=acc[:],
                    lhsT=codes[:, tokens].bitcast(FP8X4),
                    lhsT_scale=x_scales[:, tokens],
                    rhs=w_words[:, g, f, :].bitcast(FP4X4),
                    rhs_scale=w_scales[:, g, f, :],
                    start=(g == 0),
                    stop=(g == PASSES - 1),
                )
            return acc

        LAST = ROUNDS - 1
        HEADS_OF_ROUND = TILES_PER_ROUND * HEADS

        def heads_of(a):
            return slice(a * HEADS, (a + 1) * HEADS)

        def copy_kept(a, kept, result):
            nc.scalar.copy(out=result[:, heads_of(a), :NOPE], in_=kept[:].rearrange("p (h d) -> p h d", h=HEADS))

        def multiply_by_factors(r, a, rotated, products):
            j = (r * TILES_PER_ROUND + a) % TILES_PER_BATCH
            shape = [P, HEADS, ROPE, 2]
            nc.vector.tensor_tensor(
                out=products[:, heads_of(a)],
                in0=rotated[:].rearrange("p (h m) -> p h m", h=HEADS).unsqueeze(3).to_broadcast(shape),
                in1=factors[:, j].unsqueeze(1).to_broadcast(shape),
                op=MULT,
            )

        def add_products(engine, heads, products, result):
            by_pair = products[:, heads].rearrange("p t (i q) e -> p t i q e", q=2)
            engine.tensor_tensor(
                out=result[:, heads, NOPE:].rearrange("p t (i e) -> p t i e", e=2),
                in0=by_pair[:, :, :, 0, :],
                in1=by_pair[:, :, :, 1, :],
                op=ADD,
            )

        def add_and_store(r, products, result):
            b, first = divmod(r * TILES_PER_ROUND, TILES_PER_BATCH)
            if r <= LAST - FINE_ROUNDS:
                add_products(nc.gpsimd, slice(0, HEADS_OF_ROUND), products, result)
                nc.sync.dma_start(
                    out=out_by_tile[b, :, first : first + TILES_PER_ROUND, :],
                    in_=result[:].rearrange("p (a h) d -> p a (h d)", h=HEADS),
                )
                return
            for a in range(TILES_PER_ROUND):
                if (r, a) != (LAST, TILES_PER_ROUND - 1):
                    add_products(nc.vector if r == LAST else nc.gpsimd, heads_of(a), products, result)
                    nc.sync.dma_start(
                        out=out_by_tile[b, :, first + a, :], in_=result[:, heads_of(a)].rearrange("p h d -> p (h d)")
                    )
            if r != LAST:
                return
            for h in range(0, HEADS, 2):
                heads = slice(HEADS + h, HEADS + h + 2)
                add_products(nc.vector, heads, products, result)
                nc.sync.dma_start(
                    out=out_by_tile[b, :, first + 1, h * (NOPE + ROPE) : (h + 2) * (NOPE + ROPE)],
                    in_=result[:, heads].rearrange("p h d -> p (h d)"),
                )

        transpose_round(0)
        quantise_round(0)
        transpose_round(1)

        w_scales = keep.tile([P, PASSES, 2, BANK], U8, align_bytes=256)
        for g in range(PASSES):
            nc.vector.tensor_copy(
                out=w_scales[:, g].rearrange("p f n -> p (f n)").bitcast(I32).rearrange(
                    "p (f h c) -> p f h c", f=2, h=HEADS
                ),
                in_=scales_in[:, g, :].bitcast(I32).rearrange("p (h f c) -> p f h c", h=HEADS, f=2),
            )

        factors = keep.tile([P, TILES_PER_BATCH, ROPE, 2], BF16)
        by_q = factors[:].rearrange("p j (i q) e -> p (j i) q e", q=2)
        nc.scalar.copy(out=by_q[:, :, 0, :], in_=cos_sin[:])
        nc.vector.tensor_scalar_mul(out=by_q[:, :, 1, 0:1], in0=cos_sin[:, :, 1:2], scalar1=-1.0)
        nc.vector.tensor_copy(out=by_q[:, :, 1, 1:2], in_=cos_sin[:, :, 0:1])

        for r in range(ROUNDS):
            if 2 <= r < ROUNDS - 2:
                transpose_round(r + 2)
            sort_words(r + SORT_AHEAD, 1)
            banks = []
            for a in range(TILES_PER_ROUND):
                rotated = multiply(r, a, ROTATED)
                kept = multiply(r, a, KEPT)
                banks.append((kept, rotated))
                if (r, a) in ((0, 1), (1, 0)):
                    transpose_round(r + 2)
            if r + 1 < ROUNDS:
                quantise_round(r + 1)
            result = results.tile([P, HEADS_OF_ROUND, NOPE + ROPE], F32, name="result")
            products = halves.tile([P, HEADS_OF_ROUND, ROPE, 2], F32, name="products")
            copy_kept(0, banks[0][0], result)
            sort_words(r + SORT_AHEAD, 0)
            copy_kept(1, banks[1][0], result)
            for a in range(TILES_PER_ROUND):
                multiply_by_factors(r, a, banks[a][1], products)
            add_and_store(r, products, result)
